import numpy as np
import ml_dtypes


def mxq(x, axis, fmt="e4m3"):
    dtype, down = {"e4m3": (ml_dtypes.float8_e4m3fn, 7), "e5m2": (ml_dtypes.float8_e5m2, 14)}[fmt]
    v = np.moveaxis(np.asarray(x, np.float32).astype(ml_dtypes.bfloat16).astype(np.float64), axis, -1)
    blocks = v.reshape(v.shape[:-1] + (-1, 32))
    amax = np.abs(blocks).max(-1, keepdims=True)
    byte = np.maximum(np.where(amax > 0, np.frexp(amax)[1] - 1 + 127, 0) - down, 1)
    scale = np.exp2(byte - 127.0)
    codes = (blocks / scale).astype(np.float32).astype(dtype).astype(np.float64)
    return np.moveaxis((codes * scale).reshape(v.shape), -1, axis)


WIDE = False


def mx_kscale(k):
    if not WIDE:
        return np.ones(k)
    levels = np.array([10, -10, 5, -5, 0])
    if k % 512:
        return np.exp2(np.random.permutation(np.resize(levels, k // 32))).repeat(32)
    a = np.empty((k // 512, 16))
    for p in range(k // 512):
        a[p, :8] = np.random.permutation(np.resize(levels, 8))
        for g in range(8):
            far = levels[np.abs(levels - a[p, g]) >= 10]
            a[p, g + 8] = far[np.random.randint(len(far))]
    return np.exp2(a.ravel()).repeat(32)


BF16 = ml_dtypes.bfloat16


def bf(x):
    return np.asarray(x, np.float32).astype(BF16)


def f64(x):
    return np.asarray(x).astype(np.float64)


B, S, D, F, N = 2, 1024, 1024, 1024, 1024
SPARSITY = 0.1


def make_theta_sign(d1, d2, gain, row, col):
    mask = np.random.random((d1, d2)) < SPARSITY
    mag = np.abs(np.random.standard_normal((d1, d2))) * gain / np.sqrt(SPARSITY * d1)
    th = np.where(mask, mag, -mag) / row[:, None] * col
    sign = np.where(np.random.random((d1, d2)) < 0.5, -1.0, 1.0)
    return bf(th), bf(sign)


def setup_inputs():
    s, t = mx_kscale(D), mx_kscale(F)
    x = bf(np.random.standard_normal((B, S, D)) * s)
    th1, sign1 = make_theta_sign(D, F, 1.0, s, t)
    th2, sign2 = make_theta_sign(F, N, 1.4, t, np.ones(N))
    return {"x": x, "th1": th1, "sign1": sign1, "th2": th2, "sign2": sign2, "relu": 1}


def reference(x, th1, sign1, th2, sign2, relu):
    x = f64(x)
    for th, sign in ((f64(th1), f64(sign1)), (f64(th2), f64(sign2))):
        w = th * sign * (th > 0)
        x = mxq(x, 2, "e4m3") @ mxq(w, 0, "e4m3")
        if relu:
            x = np.maximum(x, 0.0)
    return x

@@ -1,0 +1,246 @@
+from contextlib import ExitStack
+
+import concourse.mybir as mybir
+from concourse.masks import make_identity
+
+F32 = mybir.dt.float32
+BF16 = mybir.dt.bfloat16
+U32 = mybir.dt.uint32
+U8 = mybir.dt.uint8
+FP8X4 = mybir.dt.float8_e4m3fn_x4
+RELU = mybir.ActivationFunctionType.Relu
+MAX = mybir.AluOpType.max
+MULT = mybir.AluOpType.mult
+
+P = 128
+PACK = 4
+HALF = 512
+WIDTH = 1024
+TILES = 16
+FLOPS = 2 * 2 * TILES * P * WIDTH * WIDTH
+
+SCALAR, VECTOR = "scalar", "vector"
+X_COPIES_ON_VECTOR = (5, 7, 10)
+TILES_BEFORE_LAYER2 = 12
+
+
+def tile_sparse_connect_kernel(tc, x, th1, sign1, th2, sign2, relu, out):
+    assert relu == 1, "both relus are always applied"
+    nc = tc.nc
+    x_blocks = x.flatten_outer_dims().rearrange("(b p j) d -> b p j d", p=P, j=4)
+    out_blocks = out.flatten_outer_dims().rearrange("(b p j) n -> b p j n", p=P, j=4)
+    w1_rows = [w.rearrange("(a p t) f -> a p t f", p=P, t=PACK) for w in (th1, sign1)]
+    w2_rows = [w.rearrange("(a p t) n -> a p t n", p=P, t=PACK) for w in (th2, sign2)]
+
+    with ExitStack() as ctx:
+        raw = ctx.enter_context(tc.tile_pool(name="raw", bufs=1))
+        keep = ctx.enter_context(tc.tile_pool(name="keep", bufs=1))
+        stage = ctx.enter_context(tc.tile_pool(name="stage", bufs=3))
+        store = ctx.enter_context(tc.tile_pool(name="store", bufs=8))
+        psum = ctx.enter_context(tc.psum_pool(name="psum", bufs=8))
+        ctx.enter_context(tc.manual_schedule())
+
+        identity = raw.tile([P, P], F32, name="identity")
+        make_identity(nc, identity[:])
+
+        x_raw = {}
+        w_raw = {}
+
+        def load_x(block, first, count):
+            t = raw.tile([P, count, WIDTH], BF16, name="x%d_%d" % (block, first))
+            nc.sync.dma_start(out=t[:], in_=x_blocks[block, :, first:first + count, :])
+            for j in range(count):
+                x_raw[4 * block + first + j] = t[:, j, :]
+
+        def load_w1(dp, fh):
+            pair = []
+            for k, rows in enumerate(w1_rows):
+                t = raw.tile([P, PACK, HALF], BF16, name="w1_%d%d%d" % (k, dp, fh))
+                nc.sync.dma_start(out=t[:], in_=rows[dp, :, :, HALF * fh:HALF * (fh + 1)])
+                pair.append(t)
+            w_raw[(1, dp, fh)] = pair
+
+        def load_w2(fh, nh):
+            pair = []
+            for k, rows in enumerate(w2_rows):
+                t = raw.tile([P, PACK, HALF], BF16, name="w2_%d%d%d" % (k, fh, nh))
+                nc.sync.dma_start(out=t[:], in_=rows[fh, :, :, HALF * nh:HALF * (nh + 1)])
+                pair.append(t)
+            w_raw[(2, fh, nh)] = pair
+
+        load_x(0, 0, 2)
+        load_w1(0, 0)
+        load_w1(1, 0)
+        load_x(0, 2, 2)
+        load_x(1, 0, 4)
+        load_x(2, 0, 4)
+        load_w1(0, 1)
+        load_x(3, 0, 4)
+        load_w1(1, 1)
+        for nh in range(2):
+            for fh in range(2):
+                load_w2(fh, nh)
+
+        def packed(name):
+            return (keep.tile([P, HALF], U32, name=name + "_words", align_bytes=64),
+                    keep.tile([P, HALF], U8, name=name + "_scales", align_bytes=64))
+
+        w_mx = {key: packed("w%d%d%d" % key) for key in sorted(w_raw)}
+        x_mx = [packed("x%d" % pair) for pair in range(TILES // 2)]
+        h_mx = {(fh, block): packed("h%d%d" % (fh, block)) for fh in range(2) for block in range(4)}
+        x_bf = {}
+        h_bf = {}
+        w_bf = {}
+        banks = {}
+
+        def new_bank(key):
+            banks[key] = psum.tile([P, HALF], F32, tag="bank", name="bank")
+            return banks[key]
+
+        def quantise(mx, first, count, values):
+            words, scales = mx
+            nc.vector.quantize_mx(out=words[:, first:first + count].bitcast(FP8X4),
+                                  scales=scales[:, first:first + count], in_=values)
+
+        def mx_pass(acc, lhs, lhs_first, rhs, rhs_first, rhs_count, start, stop):
+            nc.tensor.matmul_mx(out=acc,
+                                lhsT=lhs[0][:, lhs_first:lhs_first + P].bitcast(FP8X4),
+                                lhsT_scale=lhs[1][:, lhs_first:lhs_first + P],
+                                rhs=rhs[0][:, rhs_first:rhs_first + rhs_count].bitcast(FP8X4),
+                                rhs_scale=rhs[1][:, rhs_first:rhs_first + rhs_count],
+                                start=start, stop=stop)
+
+        def relu_out_of_psum(engine, dst, src):
+            if engine == SCALAR:
+                nc.scalar.activation(out=dst, in_=src, func=RELU)
+            else:
+                nc.vector.tensor_scalar_max(out=dst, in0=src, scalar1=0.0)
+
+        def transpose_x(first, count):
+            for i in range(first, first + count):
+                bank = new_bank(("x", i))
+                words = x_raw[i].bitcast(F32)
+                for w in range(4):
+                    dp, u = divmod(w, 2)
+                    nc.tensor.transpose(bank[:, P * w:P * (w + 1)], words[:, 2 * P * dp + u:2 * P * (dp + 1):2], identity[:])
+            for i in range(first, first + count):
+                if i % 2 == 0:
+                    x_bf[i // 2] = stage.tile([P, 2 * 2 * P * PACK], BF16, tag="x_bf", name="x_bf", align_bytes=64)
+                dst = x_bf[i // 2][:].bitcast(F32).rearrange("q (j g r u) -> q j g r u", j=2, g=2, u=2)[:, i % 2]
+                src = banks[("x", i)][:].rearrange("q (g u r) -> q g r u", g=2, u=2)
+                if i in X_COPIES_ON_VECTOR:
+                    nc.vector.tensor_copy(out=dst, in_=src)
+                else:
+                    nc.scalar.copy(out=dst, in_=src)
+
+        def quantise_x(pair):
+            quantise(x_mx[pair], 0, HALF, x_bf[pair][:])
+
+        def build_w(key, first, count):
+            if key not in w_bf:
+                w_bf[key] = stage.tile([P, HALF, PACK], BF16, tag="w_bf", name="w_bf", align_bytes=64)
+            width = P if key[0] == 1 else count
+            for c in range(first, first + count, width):
+                columns = slice(c // P, HALF, PACK) if key[0] == 1 else slice(c, c + width)
+                theta, sign = [w[:, :, columns].rearrange("q j c -> q c j") for w in w_raw[key]]
+                nc.vector.scalar_tensor_tensor(out=w_bf[key][:, c:c + width, :], in0=theta, scalar=0.0, in1=sign, op0=MAX, op1=MULT)
+
+        def quantise_w(key, first=0, count=HALF):
+            quantise(w_mx[key], first, count, w_bf[key][:, first:first + count, :].rearrange("q c t -> q (c t)"))
+
+        def build_w_in_halves(key):
+            build_w(key, 0, HALF // 2)
+            build_w(key, HALF // 2, HALF // 2)
+
+        def layer1(i, fh):
+            bank = new_bank(("h", i, fh))
+            for t in range(PACK):
+                for dp in range(2):
+                    mx_pass(bank[:, P * t:P * (t + 1)], w_mx[(1, dp, fh)], P * t,
+                            x_mx[i // 2], P * (2 * (i % 2) + dp), P, dp == 0, dp == 1)
+            if i % 4 == 0:
+                h_bf[(fh, i // 4)] = stage.tile([P, 4, P, PACK], BF16, tag="h_bf", name="h_bf", align_bytes=64, bufs=7)
+            relu_out_of_psum(SCALAR, h_bf[(fh, i // 4)][:, i % 4], bank[:].rearrange("p (t r) -> p r t", t=PACK))
+
+        def quantise_h(fh, block):
+            quantise(h_mx[(fh, block)], 0, HALF, h_bf[(fh, block)][:].rearrange("p j r t -> p (j r t)"))
+
+        def layer2(i, nh, engine):
+            bank = new_bank(("out", i, nh))
+            for fh in range(2):
+                mx_pass(bank[:], h_mx[(fh, i // 4)], P * (i % 4), w_mx[(2, fh, nh)], 0, HALF, fh == 0, fh == 1)
+            result = store.tile([P, HALF], F32, tag="result", name="result")
+            relu_out_of_psum(engine, result[:], bank[:])
+            nc.sync.dma_start(out=out_blocks[i // 4, :, i % 4, HALF * nh:HALF * (nh + 1)], in_=result[:])
+
+        def keep_tensor_engine_busy(key, count):
+            theta = w_raw[key][0]
+            bank = new_bank(("unused", key))
+            for r in range(count):
+                nc.tensor.matmul(out=bank[:], lhsT=theta[:, r % PACK, 0:P], rhs=theta[:, r % PACK, :], start=True, stop=True)
+
+        transpose_x(0, 2)
+        keep_tensor_engine_busy((1, 0, 0), 8)
+        quantise_x(0)
+        build_w((1, 0, 0), 0, HALF)
+        keep_tensor_engine_busy((1, 1, 0), 4)
+        quantise_w((1, 0, 0))
+        build_w_in_halves((1, 1, 0))
+        transpose_x(2, 2)
+        quantise_w((1, 1, 0), 0, HALF // 2)
+        quantise_w((1, 1, 0), HALF // 2, HALF // 2)
+        quantise_x(1)
+
+        layer1(0, 0)
+        layer1(1, 0)
+        transpose_x(4, 4)
+        quantise_x(2)
+        quantise_x(3)
+        build_w((1, 0, 1), 0, HALF // 2)
+        layer1(2, 0)
+        layer1(3, 0)
+        transpose_x(8, 4)
+        quantise_x(4)
+        quantise_x(5)
+        build_w((1, 0, 1), HALF // 2, HALF // 2)
+        quantise_w((1, 0, 1))
+        build_w((1, 1, 1), 0, HALF // 2)
+        for i in range(4, 8):
+            layer1(i, 0)
+        transpose_x(12, 4)
+        quantise_x(6)
+        quantise_x(7)
+        build_w((1, 1, 1), HALF // 2, HALF // 2)
+        quantise_w((1, 1, 1))
+        for i in range(8, TILES):
+            layer1(i, 0)
+
+        build_w_in_halves((2, 0, 0))
+        quantise_w((2, 0, 0))
+        for i in range(4):
+            layer1(i, 1)
+        build_w_in_halves((2, 1, 0))
+        quantise_w((2, 1, 0))
+        quantise_h(0, 0)
+        quantise_h(1, 0)
+        quantise_h(0, 1)
+        for i in range(4, TILES_BEFORE_LAYER2):
+            layer1(i, 1)
+        quantise_h(1, 1)
+        quantise_h(0, 2)
+        quantise_h(1, 2)
+        quantise_h(0, 3)
+
+        for i in range(8):
+            layer2(i, 0, SCALAR)
+        build_w_in_halves((2, 0, 1))
+        quantise_w((2, 0, 1))
+        build_w_in_halves((2, 1, 1))
+        for i in range(TILES_BEFORE_LAYER2, TILES):
+            layer1(i, 1)
+        quantise_h(1, 3)
+        quantise_w((2, 1, 1))
+        for i in range(8, TILES):
+            layer2(i, 0, SCALAR)
+        for i in range(TILES):
+            layer2(i, 1, VECTOR if i % 2 else SCALAR)

@@ -136,21 +136,27 @@ def tile_sparse_connect_kernel(tc, x, th1, sign1, th2, sign2, relu, out):
         def quantise_x(pair):
             quantise(x_mx[pair], 0, HALF, x_bf[pair][:])
 
-        def build_w(key, first, count):
+        def relu_w1(key):
+            theta = w_raw[key][0][:].rearrange("q j c -> q (j c)")
+            nc.vector.tensor_scalar_max(out=theta, in0=theta, scalar1=0.0)
+
+        def build_w1(key):
+            w_bf[key] = stage.tile([P, HALF, PACK], BF16, tag="w_bf", name="w_bf", align_bytes=64)
+            theta, sign = [w[:].rearrange("q j (m t) -> q m j t", t=PACK) for w in w_raw[key]]
+            nc.vector.tensor_tensor(out=w_bf[key][:].rearrange("q (t m) j -> q m j t", t=PACK), in0=theta, in1=sign, op=MULT)
+
+        def build_w2(key, first, count):
             if key not in w_bf:
                 w_bf[key] = stage.tile([P, HALF, PACK], BF16, tag="w_bf", name="w_bf", align_bytes=64)
-            width = P if key[0] == 1 else count
-            for c in range(first, first + count, width):
-                columns = slice(c // P, HALF, PACK) if key[0] == 1 else slice(c, c + width)
-                theta, sign = [w[:, :, columns].rearrange("q j c -> q c j") for w in w_raw[key]]
-                nc.vector.scalar_tensor_tensor(out=w_bf[key][:, c:c + width, :], in0=theta, scalar=0.0, in1=sign, op0=MAX, op1=MULT)
+            theta, sign = [w[:, :, first:first + count].rearrange("q j c -> q c j") for w in w_raw[key]]
+            nc.vector.scalar_tensor_tensor(out=w_bf[key][:, first:first + count, :], in0=theta, scalar=0.0, in1=sign, op0=MAX, op1=MULT)
 
         def quantise_w(key, first=0, count=HALF):
             quantise(w_mx[key], first, count, w_bf[key][:, first:first + count, :].rearrange("q c t -> q (c t)"))
 
-        def build_w_in_halves(key):
-            build_w(key, 0, HALF // 2)
-            build_w(key, HALF // 2, HALF // 2)
+        def build_w2_in_halves(key):
+            build_w2(key, 0, HALF // 2)
+            build_w2(key, HALF // 2, HALF // 2)
 
         def layer1(i, fh):
             bank = new_bank(("h", i, fh))
@@ -174,18 +180,20 @@ def tile_sparse_connect_kernel(tc, x, th1, sign1, th2, sign2, relu, out):
             nc.sync.dma_start(out=out_blocks[i // 4, :, i % 4, HALF * nh:HALF * (nh + 1)], in_=result[:])
 
         def keep_tensor_engine_busy(key, count):
-            theta = w_raw[key][0]
+            sign = w_raw[key][1]
             bank = new_bank(("unused", key))
             for r in range(count):
-                nc.tensor.matmul(out=bank[:], lhsT=theta[:, r % PACK, 0:P], rhs=theta[:, r % PACK, :], start=True, stop=True)
+                nc.tensor.matmul(out=bank[:], lhsT=sign[:, r % PACK, 0:P], rhs=sign[:, r % PACK, :], start=True, stop=True)
 
         transpose_x(0, 2)
         keep_tensor_engine_busy((1, 0, 0), 8)
+        relu_w1((1, 0, 0))
         quantise_x(0)
-        build_w((1, 0, 0), 0, HALF)
+        build_w1((1, 0, 0))
+        relu_w1((1, 1, 0))
         keep_tensor_engine_busy((1, 1, 0), 4)
         quantise_w((1, 0, 0))
-        build_w_in_halves((1, 1, 0))
+        build_w1((1, 1, 0))
         transpose_x(2, 2)
         quantise_w((1, 1, 0), 0, HALF // 2)
         quantise_w((1, 1, 0), HALF // 2, HALF // 2)
@@ -196,30 +204,30 @@ def tile_sparse_connect_kernel(tc, x, th1, sign1, th2, sign2, relu, out):
         transpose_x(4, 4)
         quantise_x(2)
         quantise_x(3)
-        build_w((1, 0, 1), 0, HALF // 2)
+        relu_w1((1, 0, 1))
         layer1(2, 0)
         layer1(3, 0)
         transpose_x(8, 4)
         quantise_x(4)
         quantise_x(5)
-        build_w((1, 0, 1), HALF // 2, HALF // 2)
+        build_w1((1, 0, 1))
+        relu_w1((1, 1, 1))
         quantise_w((1, 0, 1))
-        build_w((1, 1, 1), 0, HALF // 2)
         for i in range(4, 8):
             layer1(i, 0)
         transpose_x(12, 4)
         quantise_x(6)
         quantise_x(7)
-        build_w((1, 1, 1), HALF // 2, HALF // 2)
+        build_w1((1, 1, 1))
         quantise_w((1, 1, 1))
         for i in range(8, TILES):
             layer1(i, 0)
 
-        build_w_in_halves((2, 0, 0))
+        build_w2_in_halves((2, 0, 0))
         quantise_w((2, 0, 0))
         for i in range(4):
             layer1(i, 1)
-        build_w_in_halves((2, 1, 0))
+        build_w2_in_halves((2, 1, 0))
         quantise_w((2, 1, 0))
         quantise_h(0, 0)
         quantise_h(1, 0)
@@ -233,9 +241,9 @@ def tile_sparse_connect_kernel(tc, x, th1, sign1, th2, sign2, relu, out):
 
         for i in range(8):
             layer2(i, 0, SCALAR)
-        build_w_in_halves((2, 0, 1))
+        build_w2_in_halves((2, 0, 1))
         quantise_w((2, 0, 1))
-        build_w_in_halves((2, 1, 1))
+        build_w2_in_halves((2, 1, 1))
         for i in range(TILES_BEFORE_LAYER2, TILES):
             layer1(i, 1)
         quantise_h(1, 3)

@@ -20,7 +20,6 @@ TILES = 16
 FLOPS = 2 * 2 * TILES * P * WIDTH * WIDTH
 
 SCALAR, VECTOR = "scalar", "vector"
-X_COPIES_ON_VECTOR = (5, 7, 10)
 TILES_BEFORE_LAYER2 = 12
 
 
@@ -68,15 +67,15 @@ def tile_sparse_connect_kernel(tc, x, th1, sign1, th2, sign2, relu, out):
                 pair.append(t)
             w_raw[(2, fh, nh)] = pair
 
-        load_x(0, 0, 2)
         load_w1(0, 0)
+        load_x(0, 0, 2)
         load_w1(1, 0)
         load_x(0, 2, 2)
         load_x(1, 0, 4)
         load_x(2, 0, 4)
         load_w1(0, 1)
-        load_x(3, 0, 4)
         load_w1(1, 1)
+        load_x(3, 0, 4)
         for nh in range(2):
             for fh in range(2):
                 load_w2(fh, nh)
@@ -128,10 +127,7 @@ def tile_sparse_connect_kernel(tc, x, th1, sign1, th2, sign2, relu, out):
                     x_bf[i // 2] = stage.tile([P, 2 * 2 * P * PACK], BF16, tag="x_bf", name="x_bf", align_bytes=64)
                 dst = x_bf[i // 2][:].bitcast(F32).rearrange("q (j g r u) -> q j g r u", j=2, g=2, u=2)[:, i % 2]
                 src = banks[("x", i)][:].rearrange("q (g u r) -> q g r u", g=2, u=2)
-                if i in X_COPIES_ON_VECTOR:
-                    nc.vector.tensor_copy(out=dst, in_=src)
-                else:
-                    nc.scalar.copy(out=dst, in_=src)
+                nc.scalar.copy(out=dst, in_=src)
 
         def quantise_x(pair):
             quantise(x_mx[pair], 0, HALF, x_bf[pair][:])
@@ -140,10 +136,21 @@ def tile_sparse_connect_kernel(tc, x, th1, sign1, th2, sign2, relu, out):
             theta = w_raw[key][0][:].rearrange("q j c -> q (j c)")
             nc.vector.tensor_scalar_max(out=theta, in0=theta, scalar1=0.0)
 
-        def build_w1(key):
+        def build_w1(key, first=0, count=P):
+            if key not in w_bf:
+                w_bf[key] = stage.tile([P, HALF, PACK], BF16, tag="w_bf", name="w_bf", align_bytes=64)
+            ms = slice(first, first + count)
+            theta, sign = [w[:].rearrange("q j (m t) -> q m j t", t=PACK)[:, ms] for w in w_raw[key]]
+            nc.vector.tensor_tensor(out=w_bf[key][:].rearrange("q (t m) j -> q m j t", t=PACK)[:, ms], in0=theta, in1=sign, op=MULT)
+
+        def multiply_w1(key, first):
+            theta, sign = [w[:, :, PACK * first:] for w in w_raw[key]]
+            nc.vector.tensor_tensor(out=theta, in0=theta, in1=sign, op=MULT)
             w_bf[key] = stage.tile([P, HALF, PACK], BF16, tag="w_bf", name="w_bf", align_bytes=64)
-            theta, sign = [w[:].rearrange("q j (m t) -> q m j t", t=PACK) for w in w_raw[key]]
-            nc.vector.tensor_tensor(out=w_bf[key][:].rearrange("q (t m) j -> q m j t", t=PACK), in0=theta, in1=sign, op=MULT)
+
+        def lay_out_w1(key, first):
+            product = w_raw[key][0][:].rearrange("q j (m t) -> q m j t", t=PACK)[:, first:]
+            nc.scalar.copy(out=w_bf[key][:].rearrange("q (t m) j -> q m j t", t=PACK)[:, first:], in_=product)
 
         def build_w2(key, first, count):
             if key not in w_bf:
@@ -185,51 +192,52 @@ def tile_sparse_connect_kernel(tc, x, th1, sign1, th2, sign2, relu, out):
             for r in range(count):
                 nc.tensor.matmul(out=bank[:], lhsT=sign[:, r % PACK, 0:P], rhs=sign[:, r % PACK, :], start=True, stop=True)
 
-        transpose_x(0, 2)
-        keep_tensor_engine_busy((1, 0, 0), 8)
         relu_w1((1, 0, 0))
-        quantise_x(0)
-        build_w1((1, 0, 0))
+        multiply_w1((1, 0, 0), P // 2)
+        lay_out_w1((1, 0, 0), P // 2)
+        transpose_x(0, 2)
+        build_w1((1, 0, 0), 0, P // 2)
         relu_w1((1, 1, 0))
-        keep_tensor_engine_busy((1, 1, 0), 4)
-        quantise_w((1, 0, 0))
-        build_w1((1, 1, 0))
+        multiply_w1((1, 1, 0), P // 2)
+        lay_out_w1((1, 1, 0), P // 2)
+        keep_tensor_engine_busy((1, 0, 0), 6)
         transpose_x(2, 2)
-        quantise_w((1, 1, 0), 0, HALF // 2)
-        quantise_w((1, 1, 0), HALF // 2, HALF // 2)
+        keep_tensor_engine_busy((1, 1, 0), 3)
+        build_w1((1, 1, 0), 0, P // 2)
+        quantise_w((1, 0, 0))
+        quantise_x(0)
+        quantise_w((1, 1, 0))
         quantise_x(1)
 
-        layer1(0, 0)
-        layer1(1, 0)
         transpose_x(4, 4)
+        for i in range(4):
+            layer1(i, 0)
         quantise_x(2)
         quantise_x(3)
-        relu_w1((1, 0, 1))
-        layer1(2, 0)
-        layer1(3, 0)
         transpose_x(8, 4)
-        quantise_x(4)
-        quantise_x(5)
+        relu_w1((1, 0, 1))
         build_w1((1, 0, 1))
-        relu_w1((1, 1, 1))
+        quantise_x(4)
         quantise_w((1, 0, 1))
+        quantise_x(5)
         for i in range(4, 8):
             layer1(i, 0)
+        relu_w1((1, 1, 1))
         transpose_x(12, 4)
-        quantise_x(6)
-        quantise_x(7)
         build_w1((1, 1, 1))
+        quantise_x(6)
         quantise_w((1, 1, 1))
+        quantise_x(7)
         for i in range(8, TILES):
             layer1(i, 0)
 
         build_w2_in_halves((2, 0, 0))
         quantise_w((2, 0, 0))
+        build_w2_in_halves((2, 1, 0))
+        quantise_h(0, 0)
+        quantise_w((2, 1, 0))
         for i in range(4):
             layer1(i, 1)
-        build_w2_in_halves((2, 1, 0))
-        quantise_w((2, 1, 0))
-        quantise_h(0, 0)
         quantise_h(1, 0)
         quantise_h(0, 1)
         for i in range(4, TILES_BEFORE_LAYER2):

@@ -136,21 +136,10 @@ def tile_sparse_connect_kernel(tc, x, th1, sign1, th2, sign2, relu, out):
             theta = w_raw[key][0][:].rearrange("q j c -> q (j c)")
             nc.vector.tensor_scalar_max(out=theta, in0=theta, scalar1=0.0)
 
-        def build_w1(key, first=0, count=P):
-            if key not in w_bf:
-                w_bf[key] = stage.tile([P, HALF, PACK], BF16, tag="w_bf", name="w_bf", align_bytes=64)
-            ms = slice(first, first + count)
-            theta, sign = [w[:].rearrange("q j (m t) -> q m j t", t=PACK)[:, ms] for w in w_raw[key]]
-            nc.vector.tensor_tensor(out=w_bf[key][:].rearrange("q (t m) j -> q m j t", t=PACK)[:, ms], in0=theta, in1=sign, op=MULT)
-
-        def multiply_w1(key, first):
-            theta, sign = [w[:, :, PACK * first:] for w in w_raw[key]]
-            nc.vector.tensor_tensor(out=theta, in0=theta, in1=sign, op=MULT)
+        def build_w1(key):
             w_bf[key] = stage.tile([P, HALF, PACK], BF16, tag="w_bf", name="w_bf", align_bytes=64)
-
-        def lay_out_w1(key, first):
-            product = w_raw[key][0][:].rearrange("q j (m t) -> q m j t", t=PACK)[:, first:]
-            nc.scalar.copy(out=w_bf[key][:].rearrange("q (t m) j -> q m j t", t=PACK)[:, first:], in_=product)
+            theta, sign = [w[:].rearrange("q j (m t) -> q m j t", t=PACK) for w in w_raw[key]]
+            nc.vector.tensor_tensor(out=w_bf[key][:].rearrange("q (t m) j -> q m j t", t=PACK), in0=theta, in1=sign, op=MULT)
 
         def build_w2(key, first, count):
             if key not in w_bf:
@@ -193,18 +182,14 @@ def tile_sparse_connect_kernel(tc, x, th1, sign1, th2, sign2, relu, out):
                 nc.tensor.matmul(out=bank[:], lhsT=sign[:, r % PACK, 0:P], rhs=sign[:, r % PACK, :], start=True, stop=True)
 
         relu_w1((1, 0, 0))
-        multiply_w1((1, 0, 0), P // 2)
-        lay_out_w1((1, 0, 0), P // 2)
+        build_w1((1, 0, 0))
         transpose_x(0, 2)
-        build_w1((1, 0, 0), 0, P // 2)
         relu_w1((1, 1, 0))
-        multiply_w1((1, 1, 0), P // 2)
-        lay_out_w1((1, 1, 0), P // 2)
         keep_tensor_engine_busy((1, 0, 0), 6)
         transpose_x(2, 2)
         keep_tensor_engine_busy((1, 1, 0), 3)
-        build_w1((1, 1, 0), 0, P // 2)
         quantise_w((1, 0, 0))
+        build_w1((1, 1, 0))
         quantise_x(0)
         quantise_w((1, 1, 0))
         quantise_x(1)

@@ -162,7 +162,8 @@ def tile_sparse_connect_kernel(tc, x, th1, sign1, th2, sign2, relu, out):
                             x_mx[i // 2], P * (2 * (i % 2) + dp), P, dp == 0, dp == 1)
             if i % 4 == 0:
                 h_bf[(fh, i // 4)] = stage.tile([P, 4, P, PACK], BF16, tag="h_bf", name="h_bf", align_bytes=64, bufs=7)
-            relu_out_of_psum(SCALAR, h_bf[(fh, i // 4)][:, i % 4], bank[:].rearrange("p (t r) -> p r t", t=PACK))
+            relu_out_of_psum(SCALAR, h_bf[(fh, i // 4)][:, i % 4].rearrange("p (r i) t -> p r t i", i=4),
+                             bank[:].rearrange("p (t r i) -> p r t i", t=PACK, i=4))
 
         def quantise_h(fh, block):
             quantise(h_mx[(fh, block)], 0, HALF, h_bf[(fh, block)][:].rearrange("p j r t -> p (j r t)"))

@@ -186,7 +186,7 @@ def tile_sparse_connect_kernel(tc, x, th1, sign1, th2, sign2, relu, out):
         build_w1((1, 0, 0))
         transpose_x(0, 2)
         relu_w1((1, 1, 0))
-        keep_tensor_engine_busy((1, 0, 0), 6)
+        keep_tensor_engine_busy((1, 0, 0), 4)
         transpose_x(2, 2)
         keep_tensor_engine_busy((1, 1, 0), 3)
         quantise_w((1, 0, 0))
@@ -194,27 +194,38 @@ def tile_sparse_connect_kernel(tc, x, th1, sign1, th2, sign2, relu, out):
         quantise_x(0)
         quantise_w((1, 1, 0))
         quantise_x(1)
-
-        transpose_x(4, 4)
-        for i in range(4):
-            layer1(i, 0)
+        transpose_x(4, 2)
+        keep_tensor_engine_busy((1, 1, 0), 2)
+        layer1(0, 0)
+        layer1(1, 0)
         quantise_x(2)
-        quantise_x(3)
-        transpose_x(8, 4)
         relu_w1((1, 0, 1))
+        transpose_x(6, 2)
+        layer1(2, 0)
+        layer1(3, 0)
+        quantise_x(3)
         build_w1((1, 0, 1))
+        transpose_x(8, 2)
+        layer1(4, 0)
+        layer1(5, 0)
         quantise_x(4)
         quantise_w((1, 0, 1))
-        quantise_x(5)
-        for i in range(4, 8):
-            layer1(i, 0)
         relu_w1((1, 1, 1))
-        transpose_x(12, 4)
+        transpose_x(10, 2)
+        layer1(6, 0)
+        layer1(7, 0)
+        quantise_x(5)
         build_w1((1, 1, 1))
+        transpose_x(12, 2)
+        layer1(8, 0)
+        layer1(9, 0)
         quantise_x(6)
         quantise_w((1, 1, 1))
+        transpose_x(14, 2)
+        layer1(10, 0)
+        layer1(11, 0)
         quantise_x(7)
-        for i in range(8, TILES):
+        for i in range(12, TILES):
             layer1(i, 0)
 
         build_w2_in_halves((2, 0, 0))

@@ -35,7 +35,7 @@ def tile_sparse_connect_kernel(tc, x, th1, sign1, th2, sign2, relu, out):
         raw = ctx.enter_context(tc.tile_pool(name="raw", bufs=1))
         keep = ctx.enter_context(tc.tile_pool(name="keep", bufs=1))
         stage = ctx.enter_context(tc.tile_pool(name="stage", bufs=3))
-        store = ctx.enter_context(tc.tile_pool(name="store", bufs=8))
+        store = ctx.enter_context(tc.tile_pool(name="store", bufs=5))
         psum = ctx.enter_context(tc.psum_pool(name="psum", bufs=8))
         ctx.enter_context(tc.manual_schedule())
 
@@ -72,13 +72,14 @@ def tile_sparse_connect_kernel(tc, x, th1, sign1, th2, sign2, relu, out):
         load_w1(1, 0)
         load_x(0, 2, 2)
         load_x(1, 0, 4)
-        load_x(2, 0, 4)
         load_w1(0, 1)
+        load_x(2, 0, 4)
         load_w1(1, 1)
+        load_w2(0, 0)
         load_x(3, 0, 4)
-        for nh in range(2):
-            for fh in range(2):
-                load_w2(fh, nh)
+        load_w2(1, 0)
+        load_w2(0, 1)
+        load_w2(1, 1)
 
         def packed(name):
             return (keep.tile([P, HALF], U32, name=name + "_words", align_bytes=64),
@@ -90,6 +91,7 @@ def tile_sparse_connect_kernel(tc, x, th1, sign1, th2, sign2, relu, out):
         x_bf = {}
         h_bf = {}
         w_bf = {}
+        results = {}
         banks = {}
 
         def new_bank(key):
@@ -172,9 +174,14 @@ def tile_sparse_connect_kernel(tc, x, th1, sign1, th2, sign2, relu, out):
             bank = new_bank(("out", i, nh))
             for fh in range(2):
                 mx_pass(bank[:], h_mx[(fh, i // 4)], P * (i % 4), w_mx[(2, fh, nh)], 0, HALF, fh == 0, fh == 1)
-            result = store.tile([P, HALF], F32, tag="result", name="result")
-            relu_out_of_psum(engine, result[:], bank[:])
-            nc.sync.dma_start(out=out_blocks[i // 4, :, i % 4, HALF * nh:HALF * (nh + 1)], in_=result[:])
+            if i % 2 == 0:
+                results[nh] = store.tile([P, 2, HALF], F32, tag="result", name="result")
+            relu_out_of_psum(engine, results[nh][:, i % 2, :], bank[:])
+            columns = slice(HALF * nh, HALF * (nh + 1))
+            if nh == 1 and i >= TILES - 2:
+                nc.sync.dma_start(out=out_blocks[i // 4, :, i % 4, columns], in_=results[nh][:, i % 2, :])
+            elif i % 2 == 1:
+                nc.sync.dma_start(out=out_blocks[i // 4, :, i % 4 - 1:i % 4 + 1, columns], in_=results[nh][:])
 
         def keep_tensor_engine_busy(key, count):
             sign = w_raw[key][1]
@@ -203,57 +210,56 @@ def tile_sparse_connect_kernel(tc, x, th1, sign1, th2, sign2, relu, out):
         transpose_x(6, 2)
         layer1(2, 0)
         layer1(3, 0)
-        quantise_x(3)
         build_w1((1, 0, 1))
+        quantise_x(3)
         transpose_x(8, 2)
         layer1(4, 0)
         layer1(5, 0)
-        quantise_x(4)
         quantise_w((1, 0, 1))
         relu_w1((1, 1, 1))
+        quantise_x(4)
         transpose_x(10, 2)
         layer1(6, 0)
         layer1(7, 0)
-        quantise_x(5)
         build_w1((1, 1, 1))
-        transpose_x(12, 2)
-        layer1(8, 0)
-        layer1(9, 0)
-        quantise_x(6)
+        quantise_x(5)
         quantise_w((1, 1, 1))
-        transpose_x(14, 2)
-        layer1(10, 0)
-        layer1(11, 0)
-        quantise_x(7)
-        for i in range(12, TILES):
+        for i in range(8, 12):
             layer1(i, 0)
 
         build_w2_in_halves((2, 0, 0))
-        quantise_w((2, 0, 0))
-        build_w2_in_halves((2, 1, 0))
-        quantise_h(0, 0)
-        quantise_w((2, 1, 0))
         for i in range(4):
             layer1(i, 1)
-        quantise_h(1, 0)
-        quantise_h(0, 1)
-        for i in range(4, TILES_BEFORE_LAYER2):
+        quantise_h(0, 0)
+        quantise_w((2, 0, 0))
+        transpose_x(12, 2)
+        build_w2_in_halves((2, 1, 0))
+        for i in range(4, 8):
             layer1(i, 1)
+        quantise_x(6)
+        quantise_w((2, 1, 0))
+        quantise_h(1, 0)
+        transpose_x(14, 2)
+        quantise_h(0, 1)
+        for i in range(8, 12):
+            layer1(i, 1)
+        quantise_x(7)
         quantise_h(1, 1)
         quantise_h(0, 2)
         quantise_h(1, 2)
-        quantise_h(0, 3)
-
+        for i in range(12, TILES):
+            layer1(i, 0)
         for i in range(8):
             layer2(i, 0, SCALAR)
         build_w2_in_halves((2, 0, 1))
+        quantise_h(0, 3)
         quantise_w((2, 0, 1))
         build_w2_in_halves((2, 1, 1))
-        for i in range(TILES_BEFORE_LAYER2, TILES):
+        for i in range(12, TILES):
             layer1(i, 1)
         quantise_h(1, 3)
         quantise_w((2, 1, 1))
         for i in range(8, TILES):
-            layer2(i, 0, SCALAR)
+            layer2(i, 0, VECTOR if i in (11, 13, 15) else SCALAR)
         for i in range(TILES):
             layer2(i, 1, VECTOR if i % 2 else SCALAR)

@@ -17,6 +17,7 @@ PACK = 4
 HALF = 512
 WIDTH = 1024
 TILES = 16
+SINGLE_STORES = (8, 9, 14, 15)
 FLOPS = 2 * 2 * TILES * P * WIDTH * WIDTH
 
 SCALAR, VECTOR = "scalar", "vector"
@@ -76,8 +77,8 @@ def tile_sparse_connect_kernel(tc, x, th1, sign1, th2, sign2, relu, out):
         load_x(2, 0, 4)
         load_w1(1, 1)
         load_w2(0, 0)
-        load_x(3, 0, 4)
         load_w2(1, 0)
+        load_x(3, 0, 4)
         load_w2(0, 1)
         load_w2(1, 1)
 
@@ -117,13 +118,29 @@ def tile_sparse_connect_kernel(tc, x, th1, sign1, th2, sign2, relu, out):
             else:
                 nc.vector.tensor_scalar_max(out=dst, in0=src, scalar1=0.0)
 
+        x_perm = {}
+
+        def permute_x(first, count, engine=VECTOR):
+            t = stage.tile([P, count, HALF], F32, tag="x_perm", name="x_perm", bufs=2)
+            for i in range(first, first + count):
+                x_perm[i] = t[:, i - first, :]
+                dst = x_perm[i].rearrange("p (g u q) -> p g u q", g=2, u=2)
+                src = x_raw[i].bitcast(F32).rearrange("p (g q u) -> p g u q", g=2, u=2)
+                if engine == SCALAR:
+                    nc.scalar.copy(out=dst, in_=src)
+                else:
+                    nc.vector.tensor_copy(out=dst, in_=src)
+
         def transpose_x(first, count):
             for i in range(first, first + count):
                 bank = new_bank(("x", i))
-                words = x_raw[i].bitcast(F32)
                 for w in range(4):
                     dp, u = divmod(w, 2)
-                    nc.tensor.transpose(bank[:, P * w:P * (w + 1)], words[:, 2 * P * dp + u:2 * P * (dp + 1):2], identity[:])
+                    if i in x_perm:
+                        words = x_perm[i][:, P * w:P * (w + 1)]
+                    else:
+                        words = x_raw[i].bitcast(F32)[:, 2 * P * dp + u:2 * P * (dp + 1):2]
+                    nc.tensor.transpose(bank[:, P * w:P * (w + 1)], words, identity[:])
             for i in range(first, first + count):
                 if i % 2 == 0:
                     x_bf[i // 2] = stage.tile([P, 2 * 2 * P * PACK], BF16, tag="x_bf", name="x_bf", align_bytes=64)
@@ -156,7 +173,7 @@ def tile_sparse_connect_kernel(tc, x, th1, sign1, th2, sign2, relu, out):
             build_w2(key, 0, HALF // 2)
             build_w2(key, HALF // 2, HALF // 2)
 
-        def layer1(i, fh):
+        def layer1(i, fh, engine=SCALAR):
             bank = new_bank(("h", i, fh))
             for t in range(PACK):
                 for dp in range(2):
@@ -164,7 +181,7 @@ def tile_sparse_connect_kernel(tc, x, th1, sign1, th2, sign2, relu, out):
                             x_mx[i // 2], P * (2 * (i % 2) + dp), P, dp == 0, dp == 1)
             if i % 4 == 0:
                 h_bf[(fh, i // 4)] = stage.tile([P, 4, P, PACK], BF16, tag="h_bf", name="h_bf", align_bytes=64, bufs=7)
-            relu_out_of_psum(SCALAR, h_bf[(fh, i // 4)][:, i % 4].rearrange("p (r i) t -> p r t i", i=4),
+            relu_out_of_psum(engine, h_bf[(fh, i // 4)][:, i % 4].rearrange("p (r i) t -> p r t i", i=4),
                              bank[:].rearrange("p (t r i) -> p r t i", t=PACK, i=4))
 
         def quantise_h(fh, block):
@@ -178,7 +195,7 @@ def tile_sparse_connect_kernel(tc, x, th1, sign1, th2, sign2, relu, out):
                 results[nh] = store.tile([P, 2, HALF], F32, tag="result", name="result")
             relu_out_of_psum(engine, results[nh][:, i % 2, :], bank[:])
             columns = slice(HALF * nh, HALF * (nh + 1))
-            if nh == 1 and i >= TILES - 2:
+            if nh == 1 and i in SINGLE_STORES:
                 nc.sync.dma_start(out=out_blocks[i // 4, :, i % 4, columns], in_=results[nh][:, i % 2, :])
             elif i % 2 == 1:
                 nc.sync.dma_start(out=out_blocks[i // 4, :, i % 4 - 1:i % 4 + 1, columns], in_=results[nh][:])
@@ -232,34 +249,45 @@ def tile_sparse_connect_kernel(tc, x, th1, sign1, th2, sign2, relu, out):
             layer1(i, 1)
         quantise_h(0, 0)
         quantise_w((2, 0, 0))
-        transpose_x(12, 2)
         build_w2_in_halves((2, 1, 0))
         for i in range(4, 8):
             layer1(i, 1)
-        quantise_x(6)
-        quantise_w((2, 1, 0))
         quantise_h(1, 0)
-        transpose_x(14, 2)
+        quantise_w((2, 1, 0))
         quantise_h(0, 1)
         for i in range(8, 12):
             layer1(i, 1)
-        quantise_x(7)
         quantise_h(1, 1)
         quantise_h(0, 2)
         quantise_h(1, 2)
-        for i in range(12, TILES):
-            layer1(i, 0)
-        for i in range(8):
+        permute_x(12, 2)
+        permute_x(14, 2)
+
+        for i in range(4):
+            layer2(i, 0, SCALAR)
+        transpose_x(12, 2)
+        for i in range(4, 8):
             layer2(i, 0, SCALAR)
         build_w2_in_halves((2, 0, 1))
-        quantise_h(0, 3)
+        quantise_x(6)
+        transpose_x(14, 2)
+        for i in range(8, 12):
+            layer2(i, 0, SCALAR)
         quantise_w((2, 0, 1))
+        quantise_x(7)
         build_w2_in_halves((2, 1, 1))
         for i in range(12, TILES):
-            layer1(i, 1)
-        quantise_h(1, 3)
+            layer1(i, 0)
         quantise_w((2, 1, 1))
-        for i in range(8, TILES):
-            layer2(i, 0, VECTOR if i in (11, 13, 15) else SCALAR)
-        for i in range(TILES):
+        quantise_h(0, 3)
+        for i in range(8):
+            layer2(i, 1, VECTOR if i % 2 else SCALAR)
+        for i in range(12, TILES):
+            layer1(i, 1, VECTOR if i % 2 else SCALAR)
+        quantise_h(1, 3)
+        for i in range(8, 12):
+            layer2(i, 1, VECTOR if i == 11 else SCALAR)
+        for i in range(12, TILES):
+            layer2(i, 0, VECTOR if i % 2 else SCALAR)
+        for i in range(12, TILES):
             layer2(i, 1, VECTOR if i % 2 else SCALAR)

from contextlib import ExitStack

import concourse.mybir as mybir
from concourse.masks import make_identity

F32 = mybir.dt.float32
BF16 = mybir.dt.bfloat16
U32 = mybir.dt.uint32
U8 = mybir.dt.uint8
FP8X4 = mybir.dt.float8_e4m3fn_x4
RELU = mybir.ActivationFunctionType.Relu
MAX = mybir.AluOpType.max
MULT = mybir.AluOpType.mult

P = 128
PACK = 4
HALF = 512
WIDTH = 1024
TILES = 16
SINGLE_STORES = (8, 9, 14, 15)
FLOPS = 2 * 2 * TILES * P * WIDTH * WIDTH

SCALAR, VECTOR = "scalar", "vector"
TILES_BEFORE_LAYER2 = 12


def tile_sparse_connect_kernel(tc, x, th1, sign1, th2, sign2, relu, out):
    assert relu == 1, "both relus are always applied"
    nc = tc.nc
    x_blocks = x.flatten_outer_dims().rearrange("(b p j) d -> b p j d", p=P, j=4)
    out_blocks = out.flatten_outer_dims().rearrange("(b p j) n -> b p j n", p=P, j=4)
    w1_rows = [w.rearrange("(a p t) f -> a p t f", p=P, t=PACK) for w in (th1, sign1)]
    w2_rows = [w.rearrange("(a p t) n -> a p t n", p=P, t=PACK) for w in (th2, sign2)]

    with ExitStack() as ctx:
        raw = ctx.enter_context(tc.tile_pool(name="raw", bufs=1))
        keep = ctx.enter_context(tc.tile_pool(name="keep", bufs=1))
        stage = ctx.enter_context(tc.tile_pool(name="stage", bufs=3))
        store = ctx.enter_context(tc.tile_pool(name="store", bufs=5))
        psum = ctx.enter_context(tc.psum_pool(name="psum", bufs=8))
        ctx.enter_context(tc.manual_schedule())

        identity = raw.tile([P, P], F32, name="identity")
        make_identity(nc, identity[:])

        x_raw = {}
        w_raw = {}

        def load_x(block, first, count):
            t = raw.tile([P, count, WIDTH], BF16, name="x%d_%d" % (block, first))
            nc.sync.dma_start(out=t[:], in_=x_blocks[block, :, first:first + count, :])
            for j in range(count):
                x_raw[4 * block + first + j] = t[:, j, :]

        def load_w1(dp, fh):
            pair = []
            for k, rows in enumerate(w1_rows):
                t = raw.tile([P, PACK, HALF], BF16, name="w1_%d%d%d" % (k, dp, fh))
                nc.sync.dma_start(out=t[:], in_=rows[dp, :, :, HALF * fh:HALF * (fh + 1)])
                pair.append(t)
            w_raw[(1, dp, fh)] = pair

        def load_w2(fh, nh):
            pair = []
            for k, rows in enumerate(w2_rows):
                t = raw.tile([P, PACK, HALF], BF16, name="w2_%d%d%d" % (k, fh, nh))
                nc.sync.dma_start(out=t[:], in_=rows[fh, :, :, HALF * nh:HALF * (nh + 1)])
                pair.append(t)
            w_raw[(2, fh, nh)] = pair

        load_w1(0, 0)
        load_x(0, 0, 2)
        load_w1(1, 0)
        load_x(0, 2, 2)
        load_x(1, 0, 4)
        load_w1(0, 1)
        load_x(2, 0, 4)
        load_w1(1, 1)
        load_w2(0, 0)
        load_w2(1, 0)
        load_x(3, 0, 4)
        load_w2(0, 1)
        load_w2(1, 1)

        def packed(name):
            return (keep.tile([P, HALF], U32, name=name + "_words", align_bytes=64),
                    keep.tile([P, HALF], U8, name=name + "_scales", align_bytes=64))

        w_mx = {key: packed("w%d%d%d" % key) for key in sorted(w_raw)}
        x_mx = [packed("x%d" % pair) for pair in range(TILES // 2)]
        h_mx = {(fh, block): packed("h%d%d" % (fh, block)) for fh in range(2) for block in range(4)}
        x_bf = {}
        h_bf = {}
        w_bf = {}
        results = {}
        banks = {}

        def new_bank(key):
            banks[key] = psum.tile([P, HALF], F32, tag="bank", name="bank")
            return banks[key]

        def quantise(mx, first, count, values):
            words, scales = mx
            nc.vector.quantize_mx(out=words[:, first:first + count].bitcast(FP8X4),
                                  scales=scales[:, first:first + count], in_=values)

        def mx_pass(acc, lhs, lhs_first, rhs, rhs_first, rhs_count, start, stop):
            nc.tensor.matmul_mx(out=acc,
                                lhsT=lhs[0][:, lhs_first:lhs_first + P].bitcast(FP8X4),
                                lhsT_scale=lhs[1][:, lhs_first:lhs_first + P],
                                rhs=rhs[0][:, rhs_first:rhs_first + rhs_count].bitcast(FP8X4),
                                rhs_scale=rhs[1][:, rhs_first:rhs_first + rhs_count],
                                start=start, stop=stop)

        def relu_out_of_psum(engine, dst, src):
            if engine == SCALAR:
                nc.scalar.activation(out=dst, in_=src, func=RELU)
            else:
                nc.vector.tensor_scalar_max(out=dst, in0=src, scalar1=0.0)

        x_perm = {}

        def permute_x(first, count, engine=VECTOR):
            t = stage.tile([P, count, HALF], F32, tag="x_perm", name="x_perm", bufs=2)
            for i in range(first, first + count):
                x_perm[i] = t[:, i - first, :]
                dst = x_perm[i].rearrange("p (g u q) -> p g u q", g=2, u=2)
                src = x_raw[i].bitcast(F32).rearrange("p (g q u) -> p g u q", g=2, u=2)
                if engine == SCALAR:
                    nc.scalar.copy(out=dst, in_=src)
                else:
                    nc.vector.tensor_copy(out=dst, in_=src)

        def transpose_x(first, count):
            for i in range(first, first + count):
                bank = new_bank(("x", i))
                for w in range(4):
                    dp, u = divmod(w, 2)
                    if i in x_perm:
                        words = x_perm[i][:, P * w:P * (w + 1)]
                    else:
                        words = x_raw[i].bitcast(F32)[:, 2 * P * dp + u:2 * P * (dp + 1):2]
                    nc.tensor.transpose(bank[:, P * w:P * (w + 1)], words, identity[:])
            for i in range(first, first + count):
                if i % 2 == 0:
                    x_bf[i // 2] = stage.tile([P, 2 * 2 * P * PACK], BF16, tag="x_bf", name="x_bf", align_bytes=64)
                dst = x_bf[i // 2][:].bitcast(F32).rearrange("q (j g r u) -> q j g r u", j=2, g=2, u=2)[:, i % 2]
                src = banks[("x", i)][:].rearrange("q (g u r) -> q g r u", g=2, u=2)
                nc.scalar.copy(out=dst, in_=src)

        def quantise_x(pair):
            quantise(x_mx[pair], 0, HALF, x_bf[pair][:])

        def relu_w1(key):
            theta = w_raw[key][0][:].rearrange("q j c -> q (j c)")
            nc.vector.tensor_scalar_max(out=theta, in0=theta, scalar1=0.0)

        def build_w1(key):
            w_bf[key] = stage.tile([P, HALF, PACK], BF16, tag="w_bf", name="w_bf", align_bytes=64)
            theta, sign = [w[:].rearrange("q j (m t) -> q m j t", t=PACK) for w in w_raw[key]]
            nc.vector.tensor_tensor(out=w_bf[key][:].rearrange("q (t m) j -> q m j t", t=PACK), in0=theta, in1=sign, op=MULT)

        def build_w2(key, first, count):
            if key not in w_bf:
                w_bf[key] = stage.tile([P, HALF, PACK], BF16, tag="w_bf", name="w_bf", align_bytes=64)
            theta, sign = [w[:, :, first:first + count].rearrange("q j c -> q c j") for w in w_raw[key]]
            nc.vector.scalar_tensor_tensor(out=w_bf[key][:, first:first + count, :], in0=theta, scalar=0.0, in1=sign, op0=MAX, op1=MULT)

        def quantise_w(key, first=0, count=HALF):
            quantise(w_mx[key], first, count, w_bf[key][:, first:first + count, :].rearrange("q c t -> q (c t)"))

        def build_w2_in_halves(key):
            build_w2(key, 0, HALF // 2)
            build_w2(key, HALF // 2, HALF // 2)

        def layer1(i, fh, engine=SCALAR):
            bank = new_bank(("h", i, fh))
            for t in range(PACK):
                for dp in range(2):
                    mx_pass(bank[:, P * t:P * (t + 1)], w_mx[(1, dp, fh)], P * t,
                            x_mx[i // 2], P * (2 * (i % 2) + dp), P, dp == 0, dp == 1)
            if i % 4 == 0:
                h_bf[(fh, i // 4)] = stage.tile([P, 4, P, PACK], BF16, tag="h_bf", name="h_bf", align_bytes=64, bufs=7)
            relu_out_of_psum(engine, h_bf[(fh, i // 4)][:, i % 4].rearrange("p (r i) t -> p r t i", i=4),
                             bank[:].rearrange("p (t r i) -> p r t i", t=PACK, i=4))

        def quantise_h(fh, block):
            quantise(h_mx[(fh, block)], 0, HALF, h_bf[(fh, block)][:].rearrange("p j r t -> p (j r t)"))

        def layer2(i, nh, engine):
            bank = new_bank(("out", i, nh))
            for fh in range(2):
                mx_pass(bank[:], h_mx[(fh, i // 4)], P * (i % 4), w_mx[(2, fh, nh)], 0, HALF, fh == 0, fh == 1)
            if i % 2 == 0:
                results[nh] = store.tile([P, 2, HALF], F32, tag="result", name="result")
            relu_out_of_psum(engine, results[nh][:, i % 2, :], bank[:])
            columns = slice(HALF * nh, HALF * (nh + 1))
            if nh == 1 and i in SINGLE_STORES:
                nc.sync.dma_start(out=out_blocks[i // 4, :, i % 4, columns], in_=results[nh][:, i % 2, :])
            elif i % 2 == 1:
                nc.sync.dma_start(out=out_blocks[i // 4, :, i % 4 - 1:i % 4 + 1, columns], in_=results[nh][:])

        def keep_tensor_engine_busy(key, count):
            sign = w_raw[key][1]
            bank = new_bank(("unused", key))
            for r in range(count):
                nc.tensor.matmul(out=bank[:], lhsT=sign[:, r % PACK, 0:P], rhs=sign[:, r % PACK, :], start=True, stop=True)

        relu_w1((1, 0, 0))
        build_w1((1, 0, 0))
        transpose_x(0, 2)
        relu_w1((1, 1, 0))
        keep_tensor_engine_busy((1, 0, 0), 4)
        transpose_x(2, 2)
        keep_tensor_engine_busy((1, 1, 0), 3)
        quantise_w((1, 0, 0))
        build_w1((1, 1, 0))
        quantise_x(0)
        quantise_w((1, 1, 0))
        quantise_x(1)
        transpose_x(4, 2)
        keep_tensor_engine_busy((1, 1, 0), 2)
        layer1(0, 0)
        layer1(1, 0)
        quantise_x(2)
        relu_w1((1, 0, 1))
        transpose_x(6, 2)
        layer1(2, 0)
        layer1(3, 0)
        build_w1((1, 0, 1))
        quantise_x(3)
        transpose_x(8, 2)
        layer1(4, 0)
        layer1(5, 0)
        quantise_w((1, 0, 1))
        relu_w1((1, 1, 1))
        quantise_x(4)
        transpose_x(10, 2)
        layer1(6, 0)
        layer1(7, 0)
        build_w1((1, 1, 1))
        quantise_x(5)
        quantise_w((1, 1, 1))
        for i in range(8, 12):
            layer1(i, 0)

        build_w2_in_halves((2, 0, 0))
        for i in range(4):
            layer1(i, 1)
        quantise_h(0, 0)
        quantise_w((2, 0, 0))
        build_w2_in_halves((2, 1, 0))
        for i in range(4, 8):
            layer1(i, 1)
        quantise_h(1, 0)
        quantise_w((2, 1, 0))
        quantise_h(0, 1)
        for i in range(8, 12):
            layer1(i, 1)
        quantise_h(1, 1)
        quantise_h(0, 2)
        quantise_h(1, 2)
        permute_x(12, 2)
        permute_x(14, 2)

        for i in range(4):
            layer2(i, 0, SCALAR)
        transpose_x(12, 2)
        for i in range(4, 8):
            layer2(i, 0, SCALAR)
        build_w2_in_halves((2, 0, 1))
        quantise_x(6)
        transpose_x(14, 2)
        for i in range(8, 12):
            layer2(i, 0, SCALAR)
        quantise_w((2, 0, 1))
        quantise_x(7)
        build_w2_in_halves((2, 1, 1))
        for i in range(12, TILES):
            layer1(i, 0)
        quantise_w((2, 1, 1))
        quantise_h(0, 3)
        for i in range(8):
            layer2(i, 1, VECTOR if i % 2 else SCALAR)
        for i in range(12, TILES):
            layer1(i, 1, VECTOR if i % 2 else SCALAR)
        quantise_h(1, 3)
        for i in range(8, 12):
            layer2(i, 1, VECTOR if i == 11 else SCALAR)
        for i in range(12, TILES):
            layer2(i, 0, VECTOR if i % 2 else SCALAR)
        for i in range(12, TILES):
            layer2(i, 1, VECTOR if i % 2 else SCALAR)
